import numpy as np
import ml_dtypes

BF16 = ml_dtypes.bfloat16


def bf(x):
    return np.asarray(x, np.float32).astype(BF16)


def f32(x):
    return np.asarray(x, np.float32)


def f64(x):
    return np.asarray(x).astype(np.float64)


def striped(idx):
    return np.tile(idx.reshape(-1, 16).T, (8, 1))


P, S, K, R, N = 1024, 256, 16, 4, 64


def setup_inputs():
    return {"base": f32(np.random.standard_normal((P, S))), "values": f32(np.random.standard_normal((P, N))), "offs": striped(np.random.permutation(S)[:N])}


def reference(base, values, offs):
    idx = offs[:16].T.reshape(-1)
    v = f64(values)
    grouped = v.reshape(P, K, R)
    top = grouped.max(axis=-1, keepdims=True)
    keep = (grouped >= top).astype(np.float64).reshape(P, N)
    out = f64(base).copy()
    out[:, idx] = np.maximum(v, 0.0) * keep
    return out

@@ -1,0 +1,52 @@
+import concourse.mybir as mybir
+
+F32 = mybir.dt.float32
+U16 = mybir.dt.uint16
+ALU = mybir.AluOpType
+RELU = mybir.ActivationFunctionType.Relu
+INNERMOST = mybir.AxisListType.X
+
+PARTITIONS = 128
+POSITIONS = 1024
+CHANNELS = 256
+LISTED = 64
+GROUP = 4
+GROUPS = LISTED // GROUP
+BLOCKS = POSITIONS // PARTITIONS
+
+
+def tile_staticcgm_kernel(tc, base, values, offs, out):
+    nc = tc.nc
+    base_blocks = base.rearrange("(b p) c -> b p c", p=PARTITIONS)
+    values_blocks = values.rearrange("(b p) j -> b p j", p=PARTITIONS)
+    out_blocks = out.rearrange("(b p) c -> b p c", p=PARTITIONS)
+
+    with (
+        tc.tile_pool(name="held", bufs=1) as held,
+        tc.tile_pool(name="work", bufs=BLOCKS) as work,
+    ):
+        offsets = held.tile([PARTITIONS, LISTED // 16], U16, name="offsets")
+        nc.sync.dma_start(offsets[:], offs)
+
+        for b in range(BLOCKS):
+            window = work.tile([PARTITIONS, CHANNELS], F32)
+            nc.sync.dma_start(window[:], base_blocks[b])
+            vals = work.tile([PARTITIONS, GROUPS, GROUP], F32)
+            nc.sync.dma_start(vals[:], values_blocks[b].rearrange("p (q t) -> p q t", t=GROUP))
+
+            top = work.tile([PARTITIONS, GROUPS, 1], F32)
+            nc.vector.tensor_reduce(top[:], vals[:], INNERMOST, ALU.max)
+            keep = work.tile([PARTITIONS, GROUPS, GROUP], F32)
+            nc.vector.tensor_tensor(
+                keep[:], vals[:], top[:].to_broadcast([PARTITIONS, GROUPS, GROUP]), ALU.is_ge
+            )
+            relu = work.tile([PARTITIONS, GROUPS, GROUP], F32)
+            nc.scalar.activation(relu[:], vals[:], RELU)
+
+            nc.vector.tensor_tensor(
+                window[:].indirect(offsets[:]),
+                relu[:].rearrange("p q t -> p (q t)"),
+                keep[:].rearrange("p q t -> p (q t)"),
+                ALU.mult,
+            )
+            nc.sync.dma_start(out_blocks[b], window[:])

@@ -11,42 +11,38 @@ POSITIONS = 1024
 CHANNELS = 256
 LISTED = 64
 GROUP = 4
-GROUPS = LISTED // GROUP
 BLOCKS = POSITIONS // PARTITIONS
+ALL_GROUPS = BLOCKS * LISTED // GROUP
 
 
 def tile_staticcgm_kernel(tc, base, values, offs, out):
     nc = tc.nc
-    base_blocks = base.rearrange("(b p) c -> b p c", p=PARTITIONS)
-    values_blocks = values.rearrange("(b p) j -> b p j", p=PARTITIONS)
-    out_blocks = out.rearrange("(b p) c -> b p c", p=PARTITIONS)
+    base_blocks = base.rearrange("(p b) c -> b p c", b=BLOCKS)
+    out_blocks = out.rearrange("(p b) c -> b p c", b=BLOCKS)
+    values_groups = values.rearrange("(p b) (q t) -> p (b q) t", b=BLOCKS, t=GROUP)
 
-    with (
-        tc.tile_pool(name="held", bufs=1) as held,
-        tc.tile_pool(name="work", bufs=BLOCKS) as work,
-    ):
+    with tc.tile_pool(name="held", bufs=1) as held:
         offsets = held.tile([PARTITIONS, LISTED // 16], U16, name="offsets")
         nc.sync.dma_start(offsets[:], offs)
-
+        vals = held.tile([PARTITIONS, ALL_GROUPS, GROUP], F32, name="vals")
+        nc.sync.dma_start(vals[:], values_groups)
+        windows = [held.tile([PARTITIONS, CHANNELS], F32, name=f"window{b}") for b in range(BLOCKS)]
         for b in range(BLOCKS):
-            window = work.tile([PARTITIONS, CHANNELS], F32)
-            nc.sync.dma_start(window[:], base_blocks[b])
-            vals = work.tile([PARTITIONS, GROUPS, GROUP], F32)
-            nc.sync.dma_start(vals[:], values_blocks[b].rearrange("p (q t) -> p q t", t=GROUP))
+            nc.sync.dma_start(windows[b][:], base_blocks[b])
 
-            top = work.tile([PARTITIONS, GROUPS, 1], F32)
-            nc.vector.tensor_reduce(top[:], vals[:], INNERMOST, ALU.max)
-            keep = work.tile([PARTITIONS, GROUPS, GROUP], F32)
-            nc.vector.tensor_tensor(
-                keep[:], vals[:], top[:].to_broadcast([PARTITIONS, GROUPS, GROUP]), ALU.is_ge
-            )
-            relu = work.tile([PARTITIONS, GROUPS, GROUP], F32)
-            nc.scalar.activation(relu[:], vals[:], RELU)
+        top = held.tile([PARTITIONS, ALL_GROUPS, 1], F32, name="top")
+        nc.vector.tensor_reduce(top[:], vals[:], INNERMOST, ALU.max)
+        keep = held.tile([PARTITIONS, ALL_GROUPS, GROUP], F32, name="keep")
+        nc.vector.tensor_tensor(
+            keep[:], vals[:], top[:].to_broadcast([PARTITIONS, ALL_GROUPS, GROUP]), ALU.is_ge
+        )
+        relu = held.tile([PARTITIONS, ALL_GROUPS, GROUP], F32, name="relu")
+        nc.scalar.activation(relu[:], vals[:], RELU)
 
+        relu_blocks = relu[:].rearrange("p (b q) t -> p b (q t)", b=BLOCKS)
+        keep_blocks = keep[:].rearrange("p (b q) t -> p b (q t)", b=BLOCKS)
+        for b in range(BLOCKS):
             nc.vector.tensor_tensor(
-                window[:].indirect(offsets[:]),
-                relu[:].rearrange("p q t -> p (q t)"),
-                keep[:].rearrange("p q t -> p (q t)"),
-                ALU.mult,
+                windows[b][:].indirect(offsets[:]), relu_blocks[:, b], keep_blocks[:, b], ALU.mult
             )
-            nc.sync.dma_start(out_blocks[b], window[:])
+            nc.sync.dma_start(out_blocks[b], windows[b][:])

@@ -20,15 +20,16 @@ def tile_staticcgm_kernel(tc, base, values, offs, out):
     base_blocks = base.rearrange("(p b) c -> b p c", b=BLOCKS)
     out_blocks = out.rearrange("(p b) c -> b p c", b=BLOCKS)
     values_groups = values.rearrange("(p b) (q t) -> p (b q) t", b=BLOCKS, t=GROUP)
+    queues = [nc.sync, nc.scalar]
 
     with tc.tile_pool(name="held", bufs=1) as held:
         offsets = held.tile([PARTITIONS, LISTED // 16], U16, name="offsets")
         nc.sync.dma_start(offsets[:], offs)
         vals = held.tile([PARTITIONS, ALL_GROUPS, GROUP], F32, name="vals")
-        nc.sync.dma_start(vals[:], values_groups)
+        nc.scalar.dma_start(vals[:], values_groups)
         windows = [held.tile([PARTITIONS, CHANNELS], F32, name=f"window{b}") for b in range(BLOCKS)]
         for b in range(BLOCKS):
-            nc.sync.dma_start(windows[b][:], base_blocks[b])
+            queues[b % 2].dma_start(windows[b][:], base_blocks[b])
 
         top = held.tile([PARTITIONS, ALL_GROUPS, 1], F32, name="top")
         nc.vector.tensor_reduce(top[:], vals[:], INNERMOST, ALU.max)
@@ -45,4 +46,4 @@ def tile_staticcgm_kernel(tc, base, values, offs, out):
             nc.vector.tensor_tensor(
                 windows[b][:].indirect(offsets[:]), relu_blocks[:, b], keep_blocks[:, b], ALU.mult
             )
-            nc.sync.dma_start(out_blocks[b], windows[b][:])
+            queues[b % 2].dma_start(out_blocks[b], windows[b][:])

@@ -14,36 +14,44 @@ GROUP = 4
 BLOCKS = POSITIONS // PARTITIONS
 ALL_GROUPS = BLOCKS * LISTED // GROUP
 
+HALVES = 2
+PART_GROUPS = ALL_GROUPS // HALVES
+PART_BLOCKS = BLOCKS // HALVES
+
 
 def tile_staticcgm_kernel(tc, base, values, offs, out):
     nc = tc.nc
     base_blocks = base.rearrange("(p b) c -> b p c", b=BLOCKS)
     out_blocks = out.rearrange("(p b) c -> b p c", b=BLOCKS)
     values_groups = values.rearrange("(p b) (q t) -> p (b q) t", b=BLOCKS, t=GROUP)
-    queues = [nc.sync, nc.scalar]
 
     with tc.tile_pool(name="held", bufs=1) as held:
         offsets = held.tile([PARTITIONS, LISTED // 16], U16, name="offsets")
+        vals = [held.tile([PARTITIONS, PART_GROUPS, GROUP], F32, name=f"vals{h}") for h in range(HALVES)]
+        nc.sync.dma_start(vals[0][:], values_groups[:, 0:PART_GROUPS])
         nc.sync.dma_start(offsets[:], offs)
-        vals = held.tile([PARTITIONS, ALL_GROUPS, GROUP], F32, name="vals")
-        nc.scalar.dma_start(vals[:], values_groups)
+        for h in range(1, HALVES):
+            nc.sync.dma_start(vals[h][:], values_groups[:, h * PART_GROUPS : (h + 1) * PART_GROUPS])
         windows = [held.tile([PARTITIONS, CHANNELS], F32, name=f"window{b}") for b in range(BLOCKS)]
         for b in range(BLOCKS):
-            queues[b % 2].dma_start(windows[b][:], base_blocks[b])
+            nc.sync.dma_start(windows[b][:], base_blocks[b])
 
-        top = held.tile([PARTITIONS, ALL_GROUPS, 1], F32, name="top")
-        nc.vector.tensor_reduce(top[:], vals[:], INNERMOST, ALU.max)
-        keep = held.tile([PARTITIONS, ALL_GROUPS, GROUP], F32, name="keep")
-        nc.vector.tensor_tensor(
-            keep[:], vals[:], top[:].to_broadcast([PARTITIONS, ALL_GROUPS, GROUP]), ALU.is_ge
-        )
-        relu = held.tile([PARTITIONS, ALL_GROUPS, GROUP], F32, name="relu")
-        nc.scalar.activation(relu[:], vals[:], RELU)
-
-        relu_blocks = relu[:].rearrange("p (b q) t -> p b (q t)", b=BLOCKS)
-        keep_blocks = keep[:].rearrange("p (b q) t -> p b (q t)", b=BLOCKS)
-        for b in range(BLOCKS):
+        top = [held.tile([PARTITIONS, PART_GROUPS, 1], F32, name=f"top{h}") for h in range(HALVES)]
+        keep = [held.tile([PARTITIONS, PART_GROUPS, GROUP], F32, name=f"keep{h}") for h in range(HALVES)]
+        relu = [held.tile([PARTITIONS, PART_GROUPS, GROUP], F32, name=f"relu{h}") for h in range(HALVES)]
+        for h in range(HALVES):
+            nc.vector.tensor_reduce(top[h][:], vals[h][:], INNERMOST, ALU.max)
+            nc.scalar.activation(relu[h][:], vals[h][:], RELU)
+        for h in range(HALVES):
             nc.vector.tensor_tensor(
-                windows[b][:].indirect(offsets[:]), relu_blocks[:, b], keep_blocks[:, b], ALU.mult
+                keep[h][:], vals[h][:], top[h][:].to_broadcast([PARTITIONS, PART_GROUPS, GROUP]), ALU.is_ge
             )
-            queues[b % 2].dma_start(out_blocks[b], windows[b][:])
+
+        for b in range(BLOCKS):
+            h, i = divmod(b, PART_BLOCKS)
+            relu_blocks = relu[h][:].rearrange("p (b q) t -> p b (q t)", b=PART_BLOCKS)
+            keep_blocks = keep[h][:].rearrange("p (b q) t -> p b (q t)", b=PART_BLOCKS)
+            nc.vector.tensor_tensor(
+                windows[b][:].indirect(offsets[:]), relu_blocks[:, i], keep_blocks[:, i], ALU.mult
+            )
+            nc.sync.dma_start(out_blocks[b], windows[b][:])

@@ -54,4 +54,4 @@ def tile_staticcgm_kernel(tc, base, values, offs, out):
             nc.vector.tensor_tensor(
                 windows[b][:].indirect(offsets[:]), relu_blocks[:, i], keep_blocks[:, i], ALU.mult
             )
-            nc.sync.dma_start(out_blocks[b], windows[b][:])
+            nc.scalar.dma_start(out_blocks[b], windows[b][:])

@@ -14,9 +14,10 @@ GROUP = 4
 BLOCKS = POSITIONS // PARTITIONS
 ALL_GROUPS = BLOCKS * LISTED // GROUP
 
-HALVES = 2
-PART_GROUPS = ALL_GROUPS // HALVES
-PART_BLOCKS = BLOCKS // HALVES
+FIRST_BLOCKS = 2
+PART_BLOCKS = (FIRST_BLOCKS, BLOCKS - FIRST_BLOCKS)
+PART_START = (0, FIRST_BLOCKS)
+BLOCK_GROUPS = LISTED // GROUP
 
 
 def tile_staticcgm_kernel(tc, base, values, offs, out):
@@ -24,34 +25,45 @@ def tile_staticcgm_kernel(tc, base, values, offs, out):
     base_blocks = base.rearrange("(p b) c -> b p c", b=BLOCKS)
     out_blocks = out.rearrange("(p b) c -> b p c", b=BLOCKS)
     values_groups = values.rearrange("(p b) (q t) -> p (b q) t", b=BLOCKS, t=GROUP)
+    parts = range(len(PART_BLOCKS))
 
     with tc.tile_pool(name="held", bufs=1) as held:
         offsets = held.tile([PARTITIONS, LISTED // 16], U16, name="offsets")
-        vals = [held.tile([PARTITIONS, PART_GROUPS, GROUP], F32, name=f"vals{h}") for h in range(HALVES)]
-        nc.sync.dma_start(vals[0][:], values_groups[:, 0:PART_GROUPS])
+        part_shape = [[PARTITIONS, PART_BLOCKS[h] * BLOCK_GROUPS, GROUP] for h in parts]
+        vals = [held.tile(part_shape[h], F32, name=f"vals{h}") for h in parts]
+        for h in parts:
+            first_group = PART_START[h] * BLOCK_GROUPS
+            nc.sync.dma_start(vals[h][:], values_groups[:, first_group : first_group + part_shape[h][1]])
         nc.sync.dma_start(offsets[:], offs)
-        for h in range(1, HALVES):
-            nc.sync.dma_start(vals[h][:], values_groups[:, h * PART_GROUPS : (h + 1) * PART_GROUPS])
         windows = [held.tile([PARTITIONS, CHANNELS], F32, name=f"window{b}") for b in range(BLOCKS)]
         for b in range(BLOCKS):
             nc.sync.dma_start(windows[b][:], base_blocks[b])
 
-        top = [held.tile([PARTITIONS, PART_GROUPS, 1], F32, name=f"top{h}") for h in range(HALVES)]
-        keep = [held.tile([PARTITIONS, PART_GROUPS, GROUP], F32, name=f"keep{h}") for h in range(HALVES)]
-        relu = [held.tile([PARTITIONS, PART_GROUPS, GROUP], F32, name=f"relu{h}") for h in range(HALVES)]
-        for h in range(HALVES):
+        top = [held.tile([PARTITIONS, part_shape[h][1], 1], F32, name=f"top{h}") for h in parts]
+        keep = [held.tile(part_shape[h], F32, name=f"keep{h}") for h in parts]
+        relu = [held.tile(part_shape[h], F32, name=f"relu{h}") for h in parts]
+
+        def find_top(h):
             nc.vector.tensor_reduce(top[h][:], vals[h][:], INNERMOST, ALU.max)
             nc.scalar.activation(relu[h][:], vals[h][:], RELU)
-        for h in range(HALVES):
-            nc.vector.tensor_tensor(
-                keep[h][:], vals[h][:], top[h][:].to_broadcast([PARTITIONS, PART_GROUPS, GROUP]), ALU.is_ge
-            )
 
-        for b in range(BLOCKS):
-            h, i = divmod(b, PART_BLOCKS)
-            relu_blocks = relu[h][:].rearrange("p (b q) t -> p b (q t)", b=PART_BLOCKS)
-            keep_blocks = keep[h][:].rearrange("p (b q) t -> p b (q t)", b=PART_BLOCKS)
+        def find_keep(h):
+            nc.vector.tensor_tensor(keep[h][:], vals[h][:], top[h][:].to_broadcast(part_shape[h]), ALU.is_ge)
+
+        def place(b):
+            h = 0 if b < FIRST_BLOCKS else 1
+            i = b - PART_START[h]
+            relu_blocks = relu[h][:].rearrange("p (b q) t -> p b (q t)", b=PART_BLOCKS[h])
+            keep_blocks = keep[h][:].rearrange("p (b q) t -> p b (q t)", b=PART_BLOCKS[h])
             nc.vector.tensor_tensor(
                 windows[b][:].indirect(offsets[:]), relu_blocks[:, i], keep_blocks[:, i], ALU.mult
             )
             nc.scalar.dma_start(out_blocks[b], windows[b][:])
+
+        find_top(0)
+        find_top(1)
+        find_keep(0)
+        place(0)
+        find_keep(1)
+        for b in range(1, BLOCKS):
+            place(b)

@@ -15,8 +15,9 @@ BLOCKS = POSITIONS // PARTITIONS
 ALL_GROUPS = BLOCKS * LISTED // GROUP
 
 FIRST_BLOCKS = 2
-PART_BLOCKS = (FIRST_BLOCKS, BLOCKS - FIRST_BLOCKS)
-PART_START = (0, FIRST_BLOCKS)
+LOAD_BLOCKS = (FIRST_BLOCKS, BLOCKS - FIRST_BLOCKS)
+PART_BLOCKS = (FIRST_BLOCKS, LOAD_BLOCKS[1] // 2, LOAD_BLOCKS[1] // 2)
+PART_START = (0, FIRST_BLOCKS, FIRST_BLOCKS + PART_BLOCKS[1])
 BLOCK_GROUPS = LISTED // GROUP
 
 
@@ -30,10 +31,12 @@ def tile_staticcgm_kernel(tc, base, values, offs, out):
     with tc.tile_pool(name="held", bufs=1) as held:
         offsets = held.tile([PARTITIONS, LISTED // 16], U16, name="offsets")
         part_shape = [[PARTITIONS, PART_BLOCKS[h] * BLOCK_GROUPS, GROUP] for h in parts]
-        vals = [held.tile(part_shape[h], F32, name=f"vals{h}") for h in parts]
-        for h in parts:
-            first_group = PART_START[h] * BLOCK_GROUPS
-            nc.sync.dma_start(vals[h][:], values_groups[:, first_group : first_group + part_shape[h][1]])
+        loaded = [held.tile([PARTITIONS, n * BLOCK_GROUPS, GROUP], F32, name=f"values{n}") for n in LOAD_BLOCKS]
+        first_groups = FIRST_BLOCKS * BLOCK_GROUPS
+        nc.sync.dma_start(loaded[0][:], values_groups[:, :first_groups])
+        nc.sync.dma_start(loaded[1][:], values_groups[:, first_groups:])
+        half_groups = PART_BLOCKS[1] * BLOCK_GROUPS
+        vals = [loaded[0][:], loaded[1][:, :half_groups], loaded[1][:, half_groups:]]
         nc.sync.dma_start(offsets[:], offs)
         windows = [held.tile([PARTITIONS, CHANNELS], F32, name=f"window{b}") for b in range(BLOCKS)]
         for b in range(BLOCKS):
@@ -44,14 +47,14 @@ def tile_staticcgm_kernel(tc, base, values, offs, out):
         relu = [held.tile(part_shape[h], F32, name=f"relu{h}") for h in parts]
 
         def find_top(h):
-            nc.vector.tensor_reduce(top[h][:], vals[h][:], INNERMOST, ALU.max)
-            nc.scalar.activation(relu[h][:], vals[h][:], RELU)
+            nc.vector.tensor_reduce(top[h][:], vals[h], INNERMOST, ALU.max)
+            nc.scalar.activation(relu[h][:], vals[h], RELU)
 
         def find_keep(h):
-            nc.vector.tensor_tensor(keep[h][:], vals[h][:], top[h][:].to_broadcast(part_shape[h]), ALU.is_ge)
+            nc.vector.tensor_tensor(keep[h][:], vals[h], top[h][:].to_broadcast(part_shape[h]), ALU.is_ge)
 
         def place(b):
-            h = 0 if b < FIRST_BLOCKS else 1
+            h = max(part for part in parts if PART_START[part] <= b)
             i = b - PART_START[h]
             relu_blocks = relu[h][:].rearrange("p (b q) t -> p b (q t)", b=PART_BLOCKS[h])
             keep_blocks = keep[h][:].rearrange("p (b q) t -> p b (q t)", b=PART_BLOCKS[h])
@@ -60,10 +63,9 @@ def tile_staticcgm_kernel(tc, base, values, offs, out):
             )
             nc.scalar.dma_start(out_blocks[b], windows[b][:])
 
-        find_top(0)
-        find_top(1)
-        find_keep(0)
-        place(0)
-        find_keep(1)
-        for b in range(1, BLOCKS):
+        for h in parts:
+            find_top(h)
+        for h in parts:
+            find_keep(h)
+        for b in range(BLOCKS):
             place(b)

@@ -14,10 +14,10 @@ GROUP = 4
 BLOCKS = POSITIONS // PARTITIONS
 ALL_GROUPS = BLOCKS * LISTED // GROUP
 
-FIRST_BLOCKS = 2
-LOAD_BLOCKS = (FIRST_BLOCKS, BLOCKS - FIRST_BLOCKS)
-PART_BLOCKS = (FIRST_BLOCKS, LOAD_BLOCKS[1] // 2, LOAD_BLOCKS[1] // 2)
-PART_START = (0, FIRST_BLOCKS, FIRST_BLOCKS + PART_BLOCKS[1])
+LOAD_BLOCKS = (2, 6)
+PART_BLOCKS = (1, 1, 2, 2, 2)
+PART_START = tuple(sum(PART_BLOCKS[:h]) for h in range(len(PART_BLOCKS)))
+PART_LOAD = (0, 0, 1, 1, 1)
 BLOCK_GROUPS = LISTED // GROUP
 
 
@@ -32,11 +32,13 @@ def tile_staticcgm_kernel(tc, base, values, offs, out):
         offsets = held.tile([PARTITIONS, LISTED // 16], U16, name="offsets")
         part_shape = [[PARTITIONS, PART_BLOCKS[h] * BLOCK_GROUPS, GROUP] for h in parts]
         loaded = [held.tile([PARTITIONS, n * BLOCK_GROUPS, GROUP], F32, name=f"values{n}") for n in LOAD_BLOCKS]
-        first_groups = FIRST_BLOCKS * BLOCK_GROUPS
+        first_groups = LOAD_BLOCKS[0] * BLOCK_GROUPS
         nc.sync.dma_start(loaded[0][:], values_groups[:, :first_groups])
         nc.sync.dma_start(loaded[1][:], values_groups[:, first_groups:])
-        half_groups = PART_BLOCKS[1] * BLOCK_GROUPS
-        vals = [loaded[0][:], loaded[1][:, :half_groups], loaded[1][:, half_groups:]]
+        vals = []
+        for h in parts:
+            start = PART_START[h] * BLOCK_GROUPS - PART_LOAD[h] * first_groups
+            vals.append(loaded[PART_LOAD[h]][:, start : start + part_shape[h][1]])
         nc.sync.dma_start(offsets[:], offs)
         windows = [held.tile([PARTITIONS, CHANNELS], F32, name=f"window{b}") for b in range(BLOCKS)]
         for b in range(BLOCKS):

import concourse.mybir as mybir

F32 = mybir.dt.float32
U16 = mybir.dt.uint16
ALU = mybir.AluOpType
RELU = mybir.ActivationFunctionType.Relu
INNERMOST = mybir.AxisListType.X

PARTITIONS = 128
POSITIONS = 1024
CHANNELS = 256
LISTED = 64
GROUP = 4
BLOCKS = POSITIONS // PARTITIONS
ALL_GROUPS = BLOCKS * LISTED // GROUP

LOAD_BLOCKS = (2, 6)
PART_BLOCKS = (1, 1, 2, 2, 2)
PART_START = tuple(sum(PART_BLOCKS[:h]) for h in range(len(PART_BLOCKS)))
PART_LOAD = (0, 0, 1, 1, 1)
BLOCK_GROUPS = LISTED // GROUP


def tile_staticcgm_kernel(tc, base, values, offs, out):
    nc = tc.nc
    base_blocks = base.rearrange("(p b) c -> b p c", b=BLOCKS)
    out_blocks = out.rearrange("(p b) c -> b p c", b=BLOCKS)
    values_groups = values.rearrange("(p b) (q t) -> p (b q) t", b=BLOCKS, t=GROUP)
    parts = range(len(PART_BLOCKS))

    with tc.tile_pool(name="held", bufs=1) as held:
        offsets = held.tile([PARTITIONS, LISTED // 16], U16, name="offsets")
        part_shape = [[PARTITIONS, PART_BLOCKS[h] * BLOCK_GROUPS, GROUP] for h in parts]
        loaded = [held.tile([PARTITIONS, n * BLOCK_GROUPS, GROUP], F32, name=f"values{n}") for n in LOAD_BLOCKS]
        first_groups = LOAD_BLOCKS[0] * BLOCK_GROUPS
        nc.sync.dma_start(loaded[0][:], values_groups[:, :first_groups])
        nc.sync.dma_start(loaded[1][:], values_groups[:, first_groups:])
        vals = []
        for h in parts:
            start = PART_START[h] * BLOCK_GROUPS - PART_LOAD[h] * first_groups
            vals.append(loaded[PART_LOAD[h]][:, start : start + part_shape[h][1]])
        nc.sync.dma_start(offsets[:], offs)
        windows = [held.tile([PARTITIONS, CHANNELS], F32, name=f"window{b}") for b in range(BLOCKS)]
        for b in range(BLOCKS):
            nc.sync.dma_start(windows[b][:], base_blocks[b])

        top = [held.tile([PARTITIONS, part_shape[h][1], 1], F32, name=f"top{h}") for h in parts]
        keep = [held.tile(part_shape[h], F32, name=f"keep{h}") for h in parts]
        relu = [held.tile(part_shape[h], F32, name=f"relu{h}") for h in parts]

        def find_top(h):
            nc.vector.tensor_reduce(top[h][:], vals[h], INNERMOST, ALU.max)
            nc.scalar.activation(relu[h][:], vals[h], RELU)

        def find_keep(h):
            nc.vector.tensor_tensor(keep[h][:], vals[h], top[h][:].to_broadcast(part_shape[h]), ALU.is_ge)

        def place(b):
            h = max(part for part in parts if PART_START[part] <= b)
            i = b - PART_START[h]
            relu_blocks = relu[h][:].rearrange("p (b q) t -> p b (q t)", b=PART_BLOCKS[h])
            keep_blocks = keep[h][:].rearrange("p (b q) t -> p b (q t)", b=PART_BLOCKS[h])
            nc.vector.tensor_tensor(
                windows[b][:].indirect(offsets[:]), relu_blocks[:, i], keep_blocks[:, i], ALU.mult
            )
            nc.scalar.dma_start(out_blocks[b], windows[b][:])

        for h in parts:
            find_top(h)
        for h in parts:
            find_keep(h)
        for b in range(BLOCKS):
            place(b)
